import numpy as np
import ml_dtypes


def mxq(x, axis, fmt="e4m3"):
    dtype, down = {"e4m3": (ml_dtypes.float8_e4m3fn, 7), "e5m2": (ml_dtypes.float8_e5m2, 14)}[fmt]
    v = np.moveaxis(np.asarray(x, np.float32).astype(ml_dtypes.bfloat16).astype(np.float64), axis, -1)
    blocks = v.reshape(v.shape[:-1] + (-1, 32))
    amax = np.abs(blocks).max(-1, keepdims=True)
    byte = np.maximum(np.where(amax > 0, np.frexp(amax)[1] - 1 + 127, 0) - down, 1)
    scale = np.exp2(byte - 127.0)
    codes = (blocks / scale).astype(np.float32).astype(dtype).astype(np.float64)
    return np.moveaxis((codes * scale).reshape(v.shape), -1, axis)


WIDE = False


def mx_kscale(k):
    if not WIDE:
        return np.ones(k)
    levels = np.array([10, -10, 5, -5, 0])
    a = np.random.permutation(np.resize(levels, k // 512 * 4)).reshape(k // 512, 4)
    idx = np.arange(k)
    return np.exp2(a[idx // 512, idx % 128 // 32])


BF16 = ml_dtypes.bfloat16


def bf(x):
    return np.asarray(x, np.float32).astype(BF16)


def f64(x):
    return np.asarray(x).astype(np.float64)


B, C, T, H, W, AT, AF = 1, 1024, 8, 16, 16, 32, 64
D = C // 2
C2 = 2 * C
NKV = AT * AF
REP, REM = AT // T, AT % T
QS = np.sqrt(2.0 / np.sqrt(D))


def setup_inputs():
    s = mx_kscale(C2)
    sa, sv = s[:C], s[C:]
    m = np.random.standard_normal((B, C, T))[..., None, None]
    return {"v": bf((np.random.standard_normal((B, C, T, H, W)) + 0.7 * m) * sv[None, :, None, None, None]),
            "a": bf(np.random.standard_normal((B, C, AT, AF)) * sa[None, :, None, None]),
            "Wp": bf(np.random.standard_normal((D, C2)) * 0.8 * QS / np.sqrt(C) / s[None, :]),
            "bp": bf(np.random.standard_normal(D) * 0.1),
            "Wg": bf(np.random.standard_normal((D, C2)) / np.sqrt(C) / s[None, :]),
            "bg": bf(np.random.standard_normal(D) * 0.1)}


def reference(v, a, Wp, bp, Wg, bg):
    z = f64(v).mean(axis=(3, 4))
    z = np.repeat(z, REP, axis=2)
    if REM:
        z = np.concatenate([z, np.broadcast_to(z[:, :, -1:], (B, C, REM))], axis=2)
    z = np.broadcast_to(z[..., None], (B, C, AT, AF))
    av = np.concatenate([f64(a), z], axis=1).reshape(B, C2, NKV)
    avq = mxq(av, 1, "e4m3")
    phi_av = (mxq(f64(Wp), 1, "e4m3") @ avq) + f64(bp)[:, None]
    g_av = (mxq(f64(Wg), 1, "e4m3") @ avq) + f64(bg)[:, None]
    return phi_av, g_av.transpose(0, 2, 1)

@@ -1,0 +1,259 @@
+from contextlib import ExitStack
+
+import concourse.mybir as mybir
+from concourse.masks import make_identity
+
+F32 = mybir.dt.float32
+BF16 = mybir.dt.bfloat16
+I32 = mybir.dt.int32
+U32 = mybir.dt.uint32
+U8 = mybir.dt.uint8
+FP8X4 = mybir.dt.float8_e4m3fn_x4
+ADD = mybir.AluOpType.add
+MULT = mybir.AluOpType.mult
+IDENTITY = mybir.ActivationFunctionType.Identity
+
+P = 128
+C = 1024
+T = 8
+HW = 256
+N = 2048
+COLS_PER_T = N // T
+D = 512
+K_PASS = 512
+A_PASSES = C // K_PASS
+Z_PASSES = C // K_PASS
+SLABS = C // (2 * P)
+N_TILE = 512
+CHUNKS = N // N_TILE
+D_TILES = D // P
+LO = 32
+HI = HW // LO
+Z_COPIES = 16
+
+FLOPS = 2 * 2 * D * (2 * C) * N
+
+
+def tile_nlgate_pa_kernel(tc, v, a, Wp, bp, Wg, bg, out_0, out_1):
+    nc = tc.nc
+    with ExitStack() as ctx:
+        const = ctx.enter_context(tc.tile_pool(name="const", bufs=1))
+        keep = ctx.enter_context(tc.tile_pool(name="keep", bufs=1))
+        stage = ctx.enter_context(tc.tile_pool(name="stage", bufs=3))
+        outs = ctx.enter_context(tc.tile_pool(name="outs", bufs=4))
+        psum = ctx.enter_context(tc.psum_pool(name="psum", bufs=8))
+
+        ident_bf16 = const.tile([P, P], BF16)
+        make_identity(nc, ident_bf16[:])
+        ident_f32 = const.tile([P, P], F32)
+        make_identity(nc, ident_f32[:])
+        ones = const.tile([P, P], BF16)
+        nc.vector.memset(ones[:], 1.0)
+        bp_rows = const.tile([P, P], BF16)
+        nc.vector.memset(bp_rows[:], 0.0)
+        nc.scalar.dma_start(out=bp_rows[0:D_TILES, :], in_=bp.rearrange("(m p) -> m p", p=P))
+        bg_rows = const.tile([P, D], BF16)
+        nc.vector.memset(bg_rows[:], 0.0)
+        nc.scalar.dma_start(out=bg_rows[0:1, :], in_=bg.rearrange("(o d) -> o d", o=1))
+
+        v_slabs = v.rearrange("b (s p e) t h w -> p (b s) (e t h w)", s=SLABS, p=P, e=2)
+        v_raw = []
+        for s in range(SLABS):
+            v_slab = keep.tile([P, 2 * T * HW], BF16, name="v_raw%d" % s)
+            nc.sync.dma_start(out=v_slab[:], in_=v_slabs[:, s, :])
+            v_raw.append(v_slab)
+
+        w_raw = {}
+        for label, w in (("g", Wg), ("p", Wp)):
+            for h in range(2):
+                w_half = keep.tile([P, 2, 2 * C], BF16, name="w%s_raw%d" % (label, h))
+                nc.sync.dma_start(
+                    out=w_half[:],
+                    in_=w[2 * P * h : 2 * P * (h + 1), :].rearrange("(m p) k -> p m k", p=P),
+                )
+                w_raw[(label, h)] = w_half
+
+        a_slabs = a.rearrange("b (s p e) i f -> p (b s) e (i f)", s=SLABS, p=P, e=2)
+        a_raw = []
+        for c in range(CHUNKS):
+            a_chunk = keep.tile([P, SLABS, 2, N_TILE], BF16, name="a_raw%d" % c)
+            for s in range(SLABS):
+                nc.sync.dma_start(
+                    out=a_chunk[:, s, :, :], in_=a_slabs[:, s, :, N_TILE * c : N_TILE * (c + 1)]
+                )
+            a_raw.append(a_chunk)
+
+        z_sums = keep.tile([P, SLABS, 2 * T], F32)
+        for s in range(SLABS):
+            frames = v_raw[s][:].rearrange("p (f hi lo) -> p hi f lo", hi=HI, lo=LO)
+            folded = psum.tile([P, 2 * T, LO], F32, tag="bank")
+            for hi in range(HI):
+                nc.tensor.matmul(
+                    folded[:], lhsT=ident_bf16[:], rhs=frames[:, hi], start=(hi == 0), stop=(hi == HI - 1)
+                )
+            nc.vector.tensor_reduce(out=z_sums[:, s, :], in_=folded[:], axis=mybir.AxisListType.X, op=ADD)
+
+        z_grouped = keep.tile([P, Z_PASSES, T, Z_COPIES, 4], BF16, align_bytes=64)
+        for g in range(Z_PASSES):
+            nc.vector.tensor_scalar(
+                out=z_grouped[:, g],
+                in0=z_sums[:, 2 * g : 2 * g + 2, :]
+                .rearrange("p u (e t) -> p t (u e)", e=2)
+                .unsqueeze(2)
+                .to_broadcast([P, T, Z_COPIES, 4]),
+                scalar1=1.0 / HW,
+                scalar2=None,
+                op0=MULT,
+            )
+        z_codes = keep.tile([P, Z_PASSES, T * Z_COPIES], U32, align_bytes=64)
+        z_planes = keep.tile([P, Z_PASSES, T * Z_COPIES], U8, align_bytes=64)
+        nc.vector.memset(z_planes[:].bitcast(I32), 0)
+        nc.vector.quantize_mx(
+            out=z_codes[:].rearrange("p g c -> p (g c)").bitcast(FP8X4),
+            scales=z_planes[:].rearrange("p g c -> p (g c)"),
+            in_=z_grouped[:].rearrange("p g t r j -> p (g t r j)"),
+        )
+        z_wide_codes = keep.tile([P, Z_PASSES * T, P], U32, align_bytes=64)
+        z_wide_planes = keep.tile([P, Z_PASSES * T, P], U8, align_bytes=64)
+        repeats = P // Z_COPIES
+        nc.vector.tensor_copy(
+            out=z_wide_codes[:].bitcast(I32).rearrange("p s (b r) -> p s b r", b=repeats),
+            in_=z_codes[:]
+            .bitcast(I32)
+            .rearrange("p g (t r) -> p (g t) r", t=T)
+            .unsqueeze(2)
+            .to_broadcast([P, Z_PASSES * T, repeats, Z_COPIES]),
+        )
+        nc.vector.tensor_copy(
+            out=z_wide_planes[:].bitcast(I32).rearrange("p s (b r) -> p s b r", b=repeats),
+            in_=z_planes[:]
+            .bitcast(I32)
+            .rearrange("p g (t r) -> p (g t) r", t=T)
+            .unsqueeze(2)
+            .to_broadcast([P, Z_PASSES * T, repeats, Z_COPIES // 4]),
+        )
+
+        bp_flipped = psum.tile([P, P], BF16, tag="bank")
+        nc.tensor.transpose(bp_flipped[:], bp_rows[:], ident_bf16[:])
+        bp_cols = const.tile([P, D_TILES], F32)
+        nc.vector.tensor_copy(out=bp_cols[:], in_=bp_flipped[:, 0:D_TILES])
+        bg_spread = psum.tile([P, D], F32, tag="bank")
+        nc.tensor.matmul(bg_spread[:], lhsT=ones[:], rhs=bg_rows[:], start=True, stop=True)
+        bg_all = const.tile([P, D], F32)
+        nc.vector.tensor_copy(out=bg_all[:], in_=bg_spread[:])
+
+        w_codes = {}
+        w_planes = {}
+        for label in ("g", "p"):
+            w_codes[label] = keep.tile([P, A_PASSES + Z_PASSES, D], U32, align_bytes=64, name="w%s_codes" % label)
+            w_planes[label] = keep.tile([P, A_PASSES + Z_PASSES, D], U8, align_bytes=64, name="w%s_planes" % label)
+            for h in range(2):
+                words = w_raw[(label, h)][:].bitcast(F32)
+                d_cols = slice(2 * P * h, 2 * P * (h + 1))
+                for g in range(A_PASSES + Z_PASSES):
+                    flipped = psum.tile([P, 2, 2 * P], F32, tag="bank")
+                    for u in range(2):
+                        for m in range(2):
+                            first = P * (2 * g + u)
+                            nc.tensor.transpose(
+                                flipped[:, u, P * m : P * (m + 1)], words[:, m, first : first + P], ident_f32[:]
+                            )
+                    w_grouped = stage.tile([P, 2 * P, 4], BF16, align_bytes=64)
+                    nc.scalar.copy(out=w_grouped[:].bitcast(F32), in_=flipped[:].rearrange("p u d -> p d u"))
+                    nc.vector.quantize_mx(
+                        out=w_codes[label][:, g, d_cols].bitcast(FP8X4),
+                        scales=w_planes[label][:, g, d_cols],
+                        in_=w_grouped[:].rearrange("p d j -> p (d j)"),
+                    )
+
+        z_phi = psum.tile([P, D_TILES, T, Z_COPIES], F32, tag="bank")
+        for m in range(D_TILES):
+            for g in range(Z_PASSES):
+                nc.tensor.matmul_mx(
+                    out=z_phi[:, m],
+                    lhsT=w_codes["p"][:, A_PASSES + g, P * m : P * (m + 1)].bitcast(FP8X4),
+                    lhsT_scale=w_planes["p"][:, A_PASSES + g, P * m : P * (m + 1)],
+                    rhs=z_codes[:, g, :].bitcast(FP8X4),
+                    rhs_scale=z_planes[:, g, :],
+                    start=(g == 0),
+                    stop=(g == Z_PASSES - 1),
+                )
+        phi_bias = keep.tile([P, D_TILES, T], F32)
+        nc.vector.tensor_tensor(
+            out=phi_bias[:],
+            in0=z_phi[:, :, :, 0],
+            in1=bp_cols[:].unsqueeze(2).to_broadcast([P, D_TILES, T]),
+            op=ADD,
+        )
+        g_bias = keep.tile([P, T, D], F32)
+        for t in range(T):
+            z_g = psum.tile([P, D], F32, tag="bank")
+            for g in range(Z_PASSES):
+                nc.tensor.matmul_mx(
+                    out=z_g[:],
+                    lhsT=z_wide_codes[:, T * g + t, :].bitcast(FP8X4),
+                    lhsT_scale=z_wide_planes[:, T * g + t, :],
+                    rhs=w_codes["g"][:, A_PASSES + g, :].bitcast(FP8X4),
+                    rhs_scale=w_planes["g"][:, A_PASSES + g, :],
+                    start=(g == 0),
+                    stop=(g == Z_PASSES - 1),
+                )
+            nc.vector.tensor_tensor(out=g_bias[:, t, :], in0=z_g[:], in1=bg_all[:], op=ADD)
+
+        a_codes = keep.tile([P, A_PASSES, N], U32, align_bytes=64)
+        a_planes = keep.tile([P, A_PASSES, N], U8, align_bytes=64)
+        for c in range(CHUNKS):
+            n_cols = slice(N_TILE * c, N_TILE * (c + 1))
+            for g in range(A_PASSES):
+                rows = a_raw[c][:, 2 * g : 2 * g + 2, :, :].rearrange("p u e (n i) -> p n (u e) i", i=4)
+                a_grouped = stage.tile([P, N_TILE, 4], BF16, align_bytes=64)
+                spread = a_grouped[:].rearrange("p (n i) j -> p n j i", i=4)
+                if g == 0:
+                    nc.vector.tensor_copy(out=spread, in_=rows)
+                else:
+                    nc.scalar.copy(out=spread, in_=rows)
+                nc.vector.quantize_mx(
+                    out=a_codes[:, g, n_cols].bitcast(FP8X4),
+                    scales=a_planes[:, g, n_cols],
+                    in_=a_grouped[:].rearrange("p n j -> p (n j)"),
+                )
+
+            for m in range(D_TILES):
+                d_rows = slice(P * m, P * (m + 1))
+                phi_acc = psum.tile([P, N_TILE], F32, tag="bank")
+                for g in range(A_PASSES):
+                    nc.tensor.matmul_mx(
+                        out=phi_acc[:],
+                        lhsT=w_codes["p"][:, g, d_rows].bitcast(FP8X4),
+                        lhsT_scale=w_planes["p"][:, g, d_rows],
+                        rhs=a_codes[:, g, n_cols].bitcast(FP8X4),
+                        rhs_scale=a_planes[:, g, n_cols],
+                        start=(g == 0),
+                        stop=(g == A_PASSES - 1),
+                    )
+                phi_out = outs.tile([P, N_TILE], F32)
+                for half in range(N_TILE // COLS_PER_T):
+                    t = (N_TILE // COLS_PER_T) * c + half
+                    t_cols = slice(COLS_PER_T * half, COLS_PER_T * (half + 1))
+                    nc.scalar.activation(
+                        out=phi_out[:, t_cols], in_=phi_acc[:, t_cols], func=IDENTITY, bias=phi_bias[:, m, t : t + 1]
+                    )
+                nc.sync.dma_start(out=out_0[0, d_rows, n_cols], in_=phi_out[:])
+
+            for j in range(N_TILE // P):
+                n_rows = slice(N_TILE * c + P * j, N_TILE * c + P * (j + 1))
+                t = (N_TILE * c + P * j) // COLS_PER_T
+                g_acc = psum.tile([P, D], F32, tag="bank")
+                for g in range(A_PASSES):
+                    nc.tensor.matmul_mx(
+                        out=g_acc[:],
+                        lhsT=a_codes[:, g, n_rows].bitcast(FP8X4),
+                        lhsT_scale=a_planes[:, g, n_rows],
+                        rhs=w_codes["g"][:, g, :].bitcast(FP8X4),
+                        rhs_scale=w_planes["g"][:, g, :],
+                        start=(g == 0),
+                        stop=(g == A_PASSES - 1),
+                    )
+                g_out = outs.tile([P, D], F32)
+                nc.vector.tensor_tensor(out=g_out[:], in0=g_acc[:], in1=g_bias[:, t, :], op=ADD)
+                nc.sync.dma_start(out=out_1[0, n_rows, :], in_=g_out[:])

@@ -29,6 +29,7 @@ CHUNKS = N // N_TILE
 D_TILES = D // P
 LO = 32
 HI = HW // LO
+OUT_BUFS = 8
 Z_COPIES = 16
 
 FLOPS = 2 * 2 * D * (2 * C) * N
@@ -40,8 +41,9 @@ def tile_nlgate_pa_kernel(tc, v, a, Wp, bp, Wg, bg, out_0, out_1):
         const = ctx.enter_context(tc.tile_pool(name="const", bufs=1))
         keep = ctx.enter_context(tc.tile_pool(name="keep", bufs=1))
         stage = ctx.enter_context(tc.tile_pool(name="stage", bufs=3))
-        outs = ctx.enter_context(tc.tile_pool(name="outs", bufs=4))
+        outs = ctx.enter_context(tc.tile_pool(name="outs", bufs=OUT_BUFS))
         psum = ctx.enter_context(tc.psum_pool(name="psum", bufs=8))
+        ctx.enter_context(tc.manual_schedule())
 
         ident_bf16 = const.tile([P, P], BF16)
         make_identity(nc, ident_bf16[:])
@@ -55,6 +57,8 @@ def tile_nlgate_pa_kernel(tc, v, a, Wp, bp, Wg, bg, out_0, out_1):
         bg_rows = const.tile([P, D], BF16)
         nc.vector.memset(bg_rows[:], 0.0)
         nc.scalar.dma_start(out=bg_rows[0:1, :], in_=bg.rearrange("(o d) -> o d", o=1))
+        z_planes = keep.tile([P, Z_PASSES, T * Z_COPIES], U8, align_bytes=64)
+        nc.vector.memset(z_planes[:].bitcast(I32), 0)
 
         v_slabs = v.rearrange("b (s p e) t h w -> p (b s) (e t h w)", s=SLABS, p=P, e=2)
         v_raw = []
@@ -106,13 +110,21 @@ def tile_nlgate_pa_kernel(tc, v, a, Wp, bp, Wg, bg, out_0, out_1):
                 op0=MULT,
             )
         z_codes = keep.tile([P, Z_PASSES, T * Z_COPIES], U32, align_bytes=64)
-        z_planes = keep.tile([P, Z_PASSES, T * Z_COPIES], U8, align_bytes=64)
-        nc.vector.memset(z_planes[:].bitcast(I32), 0)
         nc.vector.quantize_mx(
             out=z_codes[:].rearrange("p g c -> p (g c)").bitcast(FP8X4),
             scales=z_planes[:].rearrange("p g c -> p (g c)"),
             in_=z_grouped[:].rearrange("p g t r j -> p (g t r j)"),
         )
+
+        bp_flipped = psum.tile([P, P], BF16, tag="bank")
+        nc.tensor.transpose(bp_flipped[:], bp_rows[:], ident_bf16[:])
+        bp_cols = const.tile([P, D_TILES], F32)
+        nc.vector.tensor_copy(out=bp_cols[:], in_=bp_flipped[:, 0:D_TILES])
+        bg_spread = psum.tile([P, D], F32, tag="bank")
+        nc.tensor.matmul(bg_spread[:], lhsT=ones[:], rhs=bg_rows[:], start=True, stop=True)
+        bg_all = const.tile([P, D], F32)
+        nc.vector.tensor_copy(out=bg_all[:], in_=bg_spread[:])
+
         z_wide_codes = keep.tile([P, Z_PASSES * T, P], U32, align_bytes=64)
         z_wide_planes = keep.tile([P, Z_PASSES * T, P], U8, align_bytes=64)
         repeats = P // Z_COPIES
@@ -133,60 +145,34 @@ def tile_nlgate_pa_kernel(tc, v, a, Wp, bp, Wg, bg, out_0, out_1):
             .to_broadcast([P, Z_PASSES * T, repeats, Z_COPIES // 4]),
         )
 
-        bp_flipped = psum.tile([P, P], BF16, tag="bank")
-        nc.tensor.transpose(bp_flipped[:], bp_rows[:], ident_bf16[:])
-        bp_cols = const.tile([P, D_TILES], F32)
-        nc.vector.tensor_copy(out=bp_cols[:], in_=bp_flipped[:, 0:D_TILES])
-        bg_spread = psum.tile([P, D], F32, tag="bank")
-        nc.tensor.matmul(bg_spread[:], lhsT=ones[:], rhs=bg_rows[:], start=True, stop=True)
-        bg_all = const.tile([P, D], F32)
-        nc.vector.tensor_copy(out=bg_all[:], in_=bg_spread[:])
-
         w_codes = {}
         w_planes = {}
         for label in ("g", "p"):
             w_codes[label] = keep.tile([P, A_PASSES + Z_PASSES, D], U32, align_bytes=64, name="w%s_codes" % label)
             w_planes[label] = keep.tile([P, A_PASSES + Z_PASSES, D], U8, align_bytes=64, name="w%s_planes" % label)
-            for h in range(2):
-                words = w_raw[(label, h)][:].bitcast(F32)
-                d_cols = slice(2 * P * h, 2 * P * (h + 1))
-                for g in range(A_PASSES + Z_PASSES):
-                    flipped = psum.tile([P, 2, 2 * P], F32, tag="bank")
-                    for u in range(2):
-                        for m in range(2):
-                            first = P * (2 * g + u)
-                            nc.tensor.transpose(
-                                flipped[:, u, P * m : P * (m + 1)], words[:, m, first : first + P], ident_f32[:]
-                            )
-                    w_grouped = stage.tile([P, 2 * P, 4], BF16, align_bytes=64)
-                    nc.scalar.copy(out=w_grouped[:].bitcast(F32), in_=flipped[:].rearrange("p u d -> p d u"))
-                    nc.vector.quantize_mx(
-                        out=w_codes[label][:, g, d_cols].bitcast(FP8X4),
-                        scales=w_planes[label][:, g, d_cols],
-                        in_=w_grouped[:].rearrange("p d j -> p (d j)"),
-                    )
 
-        z_phi = psum.tile([P, D_TILES, T, Z_COPIES], F32, tag="bank")
-        for m in range(D_TILES):
-            for g in range(Z_PASSES):
-                nc.tensor.matmul_mx(
-                    out=z_phi[:, m],
-                    lhsT=w_codes["p"][:, A_PASSES + g, P * m : P * (m + 1)].bitcast(FP8X4),
-                    lhsT_scale=w_planes["p"][:, A_PASSES + g, P * m : P * (m + 1)],
-                    rhs=z_codes[:, g, :].bitcast(FP8X4),
-                    rhs_scale=z_planes[:, g, :],
-                    start=(g == 0),
-                    stop=(g == Z_PASSES - 1),
+        def quantise_weight_half(label, h):
+            words = w_raw[(label, h)][:].bitcast(F32)
+            d_cols = slice(2 * P * h, 2 * P * (h + 1))
+            for g in range(A_PASSES + Z_PASSES):
+                flipped = psum.tile([P, 2, 2 * P], F32, tag="bank")
+                for u in range(2):
+                    for m in range(2):
+                        first = P * (2 * g + u)
+                        nc.tensor.transpose(
+                            flipped[:, u, P * m : P * (m + 1)], words[:, m, first : first + P], ident_f32[:]
+                        )
+                w_grouped = stage.tile([P, 2 * P, 4], BF16, align_bytes=64)
+                nc.scalar.copy(out=w_grouped[:].bitcast(F32), in_=flipped[:].rearrange("p u d -> p d u"))
+                nc.vector.quantize_mx(
+                    out=w_codes[label][:, g, d_cols].bitcast(FP8X4),
+                    scales=w_planes[label][:, g, d_cols],
+                    in_=w_grouped[:].rearrange("p d j -> p (d j)"),
                 )
-        phi_bias = keep.tile([P, D_TILES, T], F32)
-        nc.vector.tensor_tensor(
-            out=phi_bias[:],
-            in0=z_phi[:, :, :, 0],
-            in1=bp_cols[:].unsqueeze(2).to_broadcast([P, D_TILES, T]),
-            op=ADD,
-        )
+
         g_bias = keep.tile([P, T, D], F32)
-        for t in range(T):
+
+        def video_rows_for_g(t):
             z_g = psum.tile([P, D], F32, tag="bank")
             for g in range(Z_PASSES):
                 nc.tensor.matmul_mx(
@@ -200,60 +186,111 @@ def tile_nlgate_pa_kernel(tc, v, a, Wp, bp, Wg, bg, out_0, out_1):
                 )
             nc.vector.tensor_tensor(out=g_bias[:, t, :], in0=z_g[:], in1=bg_all[:], op=ADD)
 
+        phi_bias = keep.tile([P, D_TILES, T], F32)
+
+        def video_columns_for_phi():
+            z_phi = psum.tile([P, D_TILES, T, Z_COPIES], F32, tag="bank")
+            for m in range(D_TILES):
+                for g in range(Z_PASSES):
+                    nc.tensor.matmul_mx(
+                        out=z_phi[:, m],
+                        lhsT=w_codes["p"][:, A_PASSES + g, P * m : P * (m + 1)].bitcast(FP8X4),
+                        lhsT_scale=w_planes["p"][:, A_PASSES + g, P * m : P * (m + 1)],
+                        rhs=z_codes[:, g, :].bitcast(FP8X4),
+                        rhs_scale=z_planes[:, g, :],
+                        start=(g == 0),
+                        stop=(g == Z_PASSES - 1),
+                    )
+            nc.vector.tensor_tensor(
+                out=phi_bias[:],
+                in0=z_phi[:, :, :, 0],
+                in1=bp_cols[:].unsqueeze(2).to_broadcast([P, D_TILES, T]),
+                op=ADD,
+            )
+
         a_codes = keep.tile([P, A_PASSES, N], U32, align_bytes=64)
         a_planes = keep.tile([P, A_PASSES, N], U8, align_bytes=64)
-        for c in range(CHUNKS):
-            n_cols = slice(N_TILE * c, N_TILE * (c + 1))
+
+        def regroup_audio(c):
+            grouped = []
             for g in range(A_PASSES):
                 rows = a_raw[c][:, 2 * g : 2 * g + 2, :, :].rearrange("p u e (n i) -> p n (u e) i", i=4)
-                a_grouped = stage.tile([P, N_TILE, 4], BF16, align_bytes=64)
+                a_grouped = stage.tile([P, N_TILE, 4], BF16, align_bytes=64, bufs=2 * A_PASSES)
                 spread = a_grouped[:].rearrange("p (n i) j -> p n j i", i=4)
                 if g == 0:
                     nc.vector.tensor_copy(out=spread, in_=rows)
                 else:
                     nc.scalar.copy(out=spread, in_=rows)
+                grouped.append(a_grouped)
+            return grouped
+
+        def quantise_audio(c, grouped):
+            n_cols = slice(N_TILE * c, N_TILE * (c + 1))
+            for g in range(A_PASSES):
                 nc.vector.quantize_mx(
                     out=a_codes[:, g, n_cols].bitcast(FP8X4),
                     scales=a_planes[:, g, n_cols],
-                    in_=a_grouped[:].rearrange("p n j -> p (n j)"),
+                    in_=grouped[g][:].rearrange("p n j -> p (n j)"),
                 )
 
-            for m in range(D_TILES):
-                d_rows = slice(P * m, P * (m + 1))
-                phi_acc = psum.tile([P, N_TILE], F32, tag="bank")
-                for g in range(A_PASSES):
-                    nc.tensor.matmul_mx(
-                        out=phi_acc[:],
-                        lhsT=w_codes["p"][:, g, d_rows].bitcast(FP8X4),
-                        lhsT_scale=w_planes["p"][:, g, d_rows],
-                        rhs=a_codes[:, g, n_cols].bitcast(FP8X4),
-                        rhs_scale=a_planes[:, g, n_cols],
-                        start=(g == 0),
-                        stop=(g == A_PASSES - 1),
-                    )
-                phi_out = outs.tile([P, N_TILE], F32)
-                for half in range(N_TILE // COLS_PER_T):
-                    t = (N_TILE // COLS_PER_T) * c + half
-                    t_cols = slice(COLS_PER_T * half, COLS_PER_T * (half + 1))
-                    nc.scalar.activation(
-                        out=phi_out[:, t_cols], in_=phi_acc[:, t_cols], func=IDENTITY, bias=phi_bias[:, m, t : t + 1]
-                    )
-                nc.sync.dma_start(out=out_0[0, d_rows, n_cols], in_=phi_out[:])
+        def g_tile(c, j):
+            n_rows = slice(N_TILE * c + P * j, N_TILE * c + P * (j + 1))
+            t = (N_TILE * c + P * j) // COLS_PER_T
+            g_acc = psum.tile([P, D], F32, tag="bank")
+            for g in range(A_PASSES):
+                nc.tensor.matmul_mx(
+                    out=g_acc[:],
+                    lhsT=a_codes[:, g, n_rows].bitcast(FP8X4),
+                    lhsT_scale=a_planes[:, g, n_rows],
+                    rhs=w_codes["g"][:, g, :].bitcast(FP8X4),
+                    rhs_scale=w_planes["g"][:, g, :],
+                    start=(g == 0),
+                    stop=(g == A_PASSES - 1),
+                )
+            g_out = outs.tile([P, D], F32)
+            nc.vector.tensor_tensor(out=g_out[:], in0=g_acc[:], in1=g_bias[:, t, :], op=ADD)
+            nc.sync.dma_start(out=out_1[0, n_rows, :], in_=g_out[:])
 
+        def phi_tile(c, m):
+            n_cols = slice(N_TILE * c, N_TILE * (c + 1))
+            d_rows = slice(P * m, P * (m + 1))
+            phi_acc = psum.tile([P, N_TILE], F32, tag="bank")
+            for g in range(A_PASSES):
+                nc.tensor.matmul_mx(
+                    out=phi_acc[:],
+                    lhsT=w_codes["p"][:, g, d_rows].bitcast(FP8X4),
+                    lhsT_scale=w_planes["p"][:, g, d_rows],
+                    rhs=a_codes[:, g, n_cols].bitcast(FP8X4),
+                    rhs_scale=a_planes[:, g, n_cols],
+                    start=(g == 0),
+                    stop=(g == A_PASSES - 1),
+                )
+            phi_out = outs.tile([P, N_TILE], F32)
+            for half in range(N_TILE // COLS_PER_T):
+                t = (N_TILE // COLS_PER_T) * c + half
+                t_cols = slice(COLS_PER_T * half, COLS_PER_T * (half + 1))
+                nc.scalar.activation(
+                    out=phi_out[:, t_cols], in_=phi_acc[:, t_cols], func=IDENTITY, bias=phi_bias[:, m, t : t + 1]
+                )
+            nc.sync.dma_start(out=out_0[0, d_rows, n_cols], in_=phi_out[:])
+
+        quantise_weight_half("g", 0)
+        quantise_weight_half("g", 1)
+        quantise_weight_half("p", 0)
+        for t in range(T // 2):
+            video_rows_for_g(t)
+        quantise_weight_half("p", 1)
+        grouped = regroup_audio(0)
+        quantise_audio(0, grouped)
+        for t in range(T // 2, T):
+            video_rows_for_g(t)
+        video_columns_for_phi()
+        for c in range(CHUNKS):
+            if c + 1 < CHUNKS:
+                grouped = regroup_audio(c + 1)
             for j in range(N_TILE // P):
-                n_rows = slice(N_TILE * c + P * j, N_TILE * c + P * (j + 1))
-                t = (N_TILE * c + P * j) // COLS_PER_T
-                g_acc = psum.tile([P, D], F32, tag="bank")
-                for g in range(A_PASSES):
-                    nc.tensor.matmul_mx(
-                        out=g_acc[:],
-                        lhsT=a_codes[:, g, n_rows].bitcast(FP8X4),
-                        lhsT_scale=a_planes[:, g, n_rows],
-                        rhs=w_codes["g"][:, g, :].bitcast(FP8X4),
-                        rhs_scale=w_planes["g"][:, g, :],
-                        start=(g == 0),
-                        stop=(g == A_PASSES - 1),
-                    )
-                g_out = outs.tile([P, D], F32)
-                nc.vector.tensor_tensor(out=g_out[:], in0=g_acc[:], in1=g_bias[:, t, :], op=ADD)
-                nc.sync.dma_start(out=out_1[0, n_rows, :], in_=g_out[:])
+                g_tile(c, j)
+            if c + 1 < CHUNKS:
+                quantise_audio(c + 1, grouped)
+            for m in range(D_TILES):
+                phi_tile(c, m)

@@ -26,10 +26,16 @@ Z_PASSES = C // K_PASS
 SLABS = C // (2 * P)
 N_TILE = 512
 CHUNKS = N // N_TILE
+HALVES = 2
+HALF_COLS = N // HALVES
+CHUNKS_PER_HALF = CHUNKS // HALVES
+T_PER_HALF = T // HALVES
+T_PER_CHUNK = T // CHUNKS
 D_TILES = D // P
 LO = 32
 HI = HW // LO
-OUT_BUFS = 8
+G_BUFS = 10
+PHI_BUFS = 4
 Z_COPIES = 16
 
 FLOPS = 2 * 2 * D * (2 * C) * N
@@ -41,7 +47,7 @@ def tile_nlgate_pa_kernel(tc, v, a, Wp, bp, Wg, bg, out_0, out_1):
         const = ctx.enter_context(tc.tile_pool(name="const", bufs=1))
         keep = ctx.enter_context(tc.tile_pool(name="keep", bufs=1))
         stage = ctx.enter_context(tc.tile_pool(name="stage", bufs=3))
-        outs = ctx.enter_context(tc.tile_pool(name="outs", bufs=OUT_BUFS))
+        outs = ctx.enter_context(tc.tile_pool(name="outs", bufs=G_BUFS))
         psum = ctx.enter_context(tc.psum_pool(name="psum", bufs=8))
         ctx.enter_context(tc.manual_schedule())
 
@@ -68,7 +74,8 @@ def tile_nlgate_pa_kernel(tc, v, a, Wp, bp, Wg, bg, out_0, out_1):
             v_raw.append(v_slab)
 
         w_raw = {}
-        for label, w in (("g", Wg), ("p", Wp)):
+
+        def load_weight(label, w):
             for h in range(2):
                 w_half = keep.tile([P, 2, 2 * C], BF16, name="w%s_raw%d" % (label, h))
                 nc.sync.dma_start(
@@ -79,13 +86,19 @@ def tile_nlgate_pa_kernel(tc, v, a, Wp, bp, Wg, bg, out_0, out_1):
 
         a_slabs = a.rearrange("b (s p e) i f -> p (b s) e (i f)", s=SLABS, p=P, e=2)
         a_raw = []
-        for c in range(CHUNKS):
-            a_chunk = keep.tile([P, SLABS, 2, N_TILE], BF16, name="a_raw%d" % c)
+
+        def load_audio_half(h):
+            a_half = keep.tile([P, SLABS, 2, HALF_COLS], BF16, name="a_raw%d" % h)
             for s in range(SLABS):
                 nc.sync.dma_start(
-                    out=a_chunk[:, s, :, :], in_=a_slabs[:, s, :, N_TILE * c : N_TILE * (c + 1)]
+                    out=a_half[:, s, :, :], in_=a_slabs[:, s, :, HALF_COLS * h : HALF_COLS * (h + 1)]
                 )
-            a_raw.append(a_chunk)
+            a_raw.append(a_half)
+
+        load_weight("g", Wg)
+        load_audio_half(0)
+        load_weight("p", Wp)
+        load_audio_half(1)
 
         z_sums = keep.tile([P, SLABS, 2 * T], F32)
         for s in range(SLABS):
@@ -212,9 +225,11 @@ def tile_nlgate_pa_kernel(tc, v, a, Wp, bp, Wg, bg, out_0, out_1):
         a_planes = keep.tile([P, A_PASSES, N], U8, align_bytes=64)
 
         def regroup_audio(c):
+            first = N_TILE * (c % CHUNKS_PER_HALF)
+            chunk = a_raw[c // CHUNKS_PER_HALF][:, :, :, first : first + N_TILE]
             grouped = []
             for g in range(A_PASSES):
-                rows = a_raw[c][:, 2 * g : 2 * g + 2, :, :].rearrange("p u e (n i) -> p n (u e) i", i=4)
+                rows = chunk[:, 2 * g : 2 * g + 2, :, :].rearrange("p u e (n i) -> p n (u e) i", i=4)
                 a_grouped = stage.tile([P, N_TILE, 4], BF16, align_bytes=64, bufs=2 * A_PASSES)
                 spread = a_grouped[:].rearrange("p (n i) j -> p n j i", i=4)
                 if g == 0:
@@ -251,46 +266,61 @@ def tile_nlgate_pa_kernel(tc, v, a, Wp, bp, Wg, bg, out_0, out_1):
             nc.vector.tensor_tensor(out=g_out[:], in0=g_acc[:], in1=g_bias[:, t, :], op=ADD)
             nc.sync.dma_start(out=out_1[0, n_rows, :], in_=g_out[:])
 
-        def phi_tile(c, m):
-            n_cols = slice(N_TILE * c, N_TILE * (c + 1))
+        def phi_rows(h, m):
             d_rows = slice(P * m, P * (m + 1))
-            phi_acc = psum.tile([P, N_TILE], F32, tag="bank")
-            for g in range(A_PASSES):
-                nc.tensor.matmul_mx(
-                    out=phi_acc[:],
-                    lhsT=w_codes["p"][:, g, d_rows].bitcast(FP8X4),
-                    lhsT_scale=w_planes["p"][:, g, d_rows],
-                    rhs=a_codes[:, g, n_cols].bitcast(FP8X4),
-                    rhs_scale=a_planes[:, g, n_cols],
-                    start=(g == 0),
-                    stop=(g == A_PASSES - 1),
-                )
-            phi_out = outs.tile([P, N_TILE], F32)
-            for half in range(N_TILE // COLS_PER_T):
-                t = (N_TILE // COLS_PER_T) * c + half
-                t_cols = slice(COLS_PER_T * half, COLS_PER_T * (half + 1))
-                nc.scalar.activation(
-                    out=phi_out[:, t_cols], in_=phi_acc[:, t_cols], func=IDENTITY, bias=phi_bias[:, m, t : t + 1]
-                )
-            nc.sync.dma_start(out=out_0[0, d_rows, n_cols], in_=phi_out[:])
+            phi_out = outs.tile([P, T_PER_HALF, COLS_PER_T], F32, bufs=PHI_BUFS)
+            for c in range(CHUNKS_PER_HALF * h, CHUNKS_PER_HALF * (h + 1)):
+                n_cols = slice(N_TILE * c, N_TILE * (c + 1))
+                phi_acc = psum.tile([P, T_PER_CHUNK, COLS_PER_T], F32, tag="bank")
+                for g in range(A_PASSES):
+                    nc.tensor.matmul_mx(
+                        out=phi_acc[:].rearrange("p t n -> p (t n)"),
+                        lhsT=w_codes["p"][:, g, d_rows].bitcast(FP8X4),
+                        lhsT_scale=w_planes["p"][:, g, d_rows],
+                        rhs=a_codes[:, g, n_cols].bitcast(FP8X4),
+                        rhs_scale=a_planes[:, g, n_cols],
+                        start=(g == 0),
+                        stop=(g == A_PASSES - 1),
+                    )
+                for i in range(T_PER_CHUNK):
+                    t = T_PER_CHUNK * c + i
+                    nc.scalar.activation(
+                        out=phi_out[:, t - T_PER_HALF * h, :],
+                        in_=phi_acc[:, i, :],
+                        func=IDENTITY,
+                        bias=phi_bias[:, m, t : t + 1],
+                    )
+            nc.sync.dma_start(
+                out=out_0[0, d_rows, HALF_COLS * h : HALF_COLS * (h + 1)],
+                in_=phi_out[:].rearrange("p t n -> p (t n)"),
+            )
+
+        def g_tiles(c):
+            for j in range(N_TILE // P):
+                g_tile(c, j)
 
         quantise_weight_half("g", 0)
         quantise_weight_half("g", 1)
-        quantise_weight_half("p", 0)
-        for t in range(T // 2):
+        for t in range(T_PER_HALF):
             video_rows_for_g(t)
-        quantise_weight_half("p", 1)
         grouped = regroup_audio(0)
         quantise_audio(0, grouped)
-        for t in range(T // 2, T):
-            video_rows_for_g(t)
+        grouped = regroup_audio(1)
+        g_tiles(0)
+        quantise_audio(1, grouped)
+        g_tiles(1)
+        quantise_weight_half("p", 0)
+        quantise_weight_half("p", 1)
         video_columns_for_phi()
-        for c in range(CHUNKS):
-            if c + 1 < CHUNKS:
-                grouped = regroup_audio(c + 1)
-            for j in range(N_TILE // P):
-                g_tile(c, j)
-            if c + 1 < CHUNKS:
-                quantise_audio(c + 1, grouped)
-            for m in range(D_TILES):
-                phi_tile(c, m)
+        for t in range(T_PER_HALF, T):
+            video_rows_for_g(t)
+        grouped = regroup_audio(2)
+        quantise_audio(2, grouped)
+        for m in range(D_TILES):
+            phi_rows(0, m)
+        grouped = regroup_audio(3)
+        g_tiles(2)
+        quantise_audio(3, grouped)
+        g_tiles(3)
+        for m in range(D_TILES):
+            phi_rows(1, m)

@@ -26,17 +26,17 @@ Z_PASSES = C // K_PASS
 SLABS = C // (2 * P)
 N_TILE = 512
 CHUNKS = N // N_TILE
-HALVES = 2
-HALF_COLS = N // HALVES
-CHUNKS_PER_HALF = CHUNKS // HALVES
-T_PER_HALF = T // HALVES
-T_PER_CHUNK = T // CHUNKS
 D_TILES = D // P
 LO = 32
 HI = HW // LO
-G_BUFS = 10
-PHI_BUFS = 4
+PHI_BUFS = 8
+G_BUFS = 3
+W_BUFS = 5
+A_BUFS = 2 * A_PASSES
+PSUM_BANKS = 8
 Z_COPIES = 16
+T_PER_CHUNK = N_TILE // COLS_PER_T
+J = N_TILE // P
 
 FLOPS = 2 * 2 * D * (2 * C) * N
 
@@ -46,25 +46,15 @@ def tile_nlgate_pa_kernel(tc, v, a, Wp, bp, Wg, bg, out_0, out_1):
     with ExitStack() as ctx:
         const = ctx.enter_context(tc.tile_pool(name="const", bufs=1))
         keep = ctx.enter_context(tc.tile_pool(name="keep", bufs=1))
-        stage = ctx.enter_context(tc.tile_pool(name="stage", bufs=3))
-        outs = ctx.enter_context(tc.tile_pool(name="outs", bufs=G_BUFS))
-        psum = ctx.enter_context(tc.psum_pool(name="psum", bufs=8))
+        stage = ctx.enter_context(tc.tile_pool(name="stage", bufs=W_BUFS))
+        outs = ctx.enter_context(tc.tile_pool(name="outs", bufs=PHI_BUFS))
+        psum = ctx.enter_context(tc.psum_pool(name="psum", bufs=PSUM_BANKS))
         ctx.enter_context(tc.manual_schedule())
 
-        ident_bf16 = const.tile([P, P], BF16)
-        make_identity(nc, ident_bf16[:])
-        ident_f32 = const.tile([P, P], F32)
-        make_identity(nc, ident_f32[:])
-        ones = const.tile([P, P], BF16)
-        nc.vector.memset(ones[:], 1.0)
-        bp_rows = const.tile([P, P], BF16)
-        nc.vector.memset(bp_rows[:], 0.0)
-        nc.scalar.dma_start(out=bp_rows[0:D_TILES, :], in_=bp.rearrange("(m p) -> m p", p=P))
-        bg_rows = const.tile([P, D], BF16)
-        nc.vector.memset(bg_rows[:], 0.0)
-        nc.scalar.dma_start(out=bg_rows[0:1, :], in_=bg.rearrange("(o d) -> o d", o=1))
-        z_planes = keep.tile([P, Z_PASSES, T * Z_COPIES], U8, align_bytes=64)
-        nc.vector.memset(z_planes[:].bitcast(I32), 0)
+        bias_rows = const.tile([P, P], BF16)
+        nc.vector.memset(bias_rows[:], 0.0)
+        nc.sync.dma_start(out=bias_rows[0:D_TILES, :], in_=bp.rearrange("(m p) -> m p", p=P))
+        nc.sync.dma_start(out=bias_rows[D_TILES : 2 * D_TILES, :], in_=bg.rearrange("(m p) -> m p", p=P))
 
         v_slabs = v.rearrange("b (s p e) t h w -> p (b s) (e t h w)", s=SLABS, p=P, e=2)
         v_raw = []
@@ -76,87 +66,52 @@ def tile_nlgate_pa_kernel(tc, v, a, Wp, bp, Wg, bg, out_0, out_1):
         w_raw = {}
 
         def load_weight(label, w):
-            for h in range(2):
-                w_half = keep.tile([P, 2, 2 * C], BF16, name="w%s_raw%d" % (label, h))
+            for half in range(2):
+                w_half = keep.tile([P, 2, 2 * C], BF16, name="w%s_raw%d" % (label, half))
                 nc.sync.dma_start(
                     out=w_half[:],
-                    in_=w[2 * P * h : 2 * P * (h + 1), :].rearrange("(m p) k -> p m k", p=P),
+                    in_=w[2 * P * half : 2 * P * (half + 1), :].rearrange("(p m) k -> p m k", m=2),
                 )
-                w_raw[(label, h)] = w_half
+                w_raw[(label, half)] = w_half
 
-        a_slabs = a.rearrange("b (s p e) i f -> p (b s) e (i f)", s=SLABS, p=P, e=2)
+        a_slabs = a.rearrange("b (s p e) at af -> p (b s) e (at af)", s=SLABS, p=P, e=2)
         a_raw = []
 
-        def load_audio_half(h):
-            a_half = keep.tile([P, SLABS, 2, HALF_COLS], BF16, name="a_raw%d" % h)
+        def load_audio(c):
+            a_chunk = keep.tile([P, SLABS, 2, N_TILE], BF16, name="a_raw%d" % c)
             for s in range(SLABS):
                 nc.sync.dma_start(
-                    out=a_half[:, s, :, :], in_=a_slabs[:, s, :, HALF_COLS * h : HALF_COLS * (h + 1)]
+                    out=a_chunk[:, s, :, :], in_=a_slabs[:, s, :, N_TILE * c : N_TILE * (c + 1)]
                 )
-            a_raw.append(a_half)
+            a_raw.append(a_chunk)
 
         load_weight("g", Wg)
-        load_audio_half(0)
+        load_audio(0)
         load_weight("p", Wp)
-        load_audio_half(1)
+        for c in range(1, CHUNKS):
+            load_audio(c)
 
-        z_sums = keep.tile([P, SLABS, 2 * T], F32)
-        for s in range(SLABS):
-            frames = v_raw[s][:].rearrange("p (f hi lo) -> p hi f lo", hi=HI, lo=LO)
-            folded = psum.tile([P, 2 * T, LO], F32, tag="bank")
-            for hi in range(HI):
-                nc.tensor.matmul(
-                    folded[:], lhsT=ident_bf16[:], rhs=frames[:, hi], start=(hi == 0), stop=(hi == HI - 1)
-                )
-            nc.vector.tensor_reduce(out=z_sums[:, s, :], in_=folded[:], axis=mybir.AxisListType.X, op=ADD)
+        ident_bf16 = const.tile([P, P], BF16)
+        make_identity(nc, ident_bf16[:])
+        ident_f32 = const.tile([P, P], F32)
+        make_identity(nc, ident_f32[:])
 
-        z_grouped = keep.tile([P, Z_PASSES, T, Z_COPIES, 4], BF16, align_bytes=64)
-        for g in range(Z_PASSES):
-            nc.vector.tensor_scalar(
-                out=z_grouped[:, g],
-                in0=z_sums[:, 2 * g : 2 * g + 2, :]
-                .rearrange("p u (e t) -> p t (u e)", e=2)
-                .unsqueeze(2)
-                .to_broadcast([P, T, Z_COPIES, 4]),
-                scalar1=1.0 / HW,
-                scalar2=None,
-                op0=MULT,
-            )
-        z_codes = keep.tile([P, Z_PASSES, T * Z_COPIES], U32, align_bytes=64)
-        nc.vector.quantize_mx(
-            out=z_codes[:].rearrange("p g c -> p (g c)").bitcast(FP8X4),
-            scales=z_planes[:].rearrange("p g c -> p (g c)"),
-            in_=z_grouped[:].rearrange("p g t r j -> p (g t r j)"),
-        )
-
-        bp_flipped = psum.tile([P, P], BF16, tag="bank")
-        nc.tensor.transpose(bp_flipped[:], bp_rows[:], ident_bf16[:])
-        bp_cols = const.tile([P, D_TILES], F32)
-        nc.vector.tensor_copy(out=bp_cols[:], in_=bp_flipped[:, 0:D_TILES])
-        bg_spread = psum.tile([P, D], F32, tag="bank")
-        nc.tensor.matmul(bg_spread[:], lhsT=ones[:], rhs=bg_rows[:], start=True, stop=True)
+        bias_cols = const.tile([P, 2 * D_TILES], F32)
+        bp_cols = bias_cols[:, 0:D_TILES]
         bg_all = const.tile([P, D], F32)
-        nc.vector.tensor_copy(out=bg_all[:], in_=bg_spread[:])
 
-        z_wide_codes = keep.tile([P, Z_PASSES * T, P], U32, align_bytes=64)
-        z_wide_planes = keep.tile([P, Z_PASSES * T, P], U8, align_bytes=64)
-        repeats = P // Z_COPIES
-        nc.vector.tensor_copy(
-            out=z_wide_codes[:].bitcast(I32).rearrange("p s (b r) -> p s b r", b=repeats),
-            in_=z_codes[:]
-            .bitcast(I32)
-            .rearrange("p g (t r) -> p (g t) r", t=T)
-            .unsqueeze(2)
-            .to_broadcast([P, Z_PASSES * T, repeats, Z_COPIES]),
-        )
-        nc.vector.tensor_copy(
-            out=z_wide_planes[:].bitcast(I32).rearrange("p s (b r) -> p s b r", b=repeats),
-            in_=z_planes[:]
-            .bitcast(I32)
-            .rearrange("p g (t r) -> p (g t) r", t=T)
-            .unsqueeze(2)
-            .to_broadcast([P, Z_PASSES * T, repeats, Z_COPIES // 4]),
-        )
+        def spread_biases():
+            bias_flipped = psum.tile([P, P], BF16, tag="bank")
+            nc.tensor.transpose(bias_flipped[:], bias_rows[:], ident_bf16[:])
+            nc.vector.tensor_copy(out=bias_cols[:], in_=bias_flipped[:, 0 : 2 * D_TILES])
+            bg_wide = const.tile([P, D_TILES, P], F32)
+            nc.vector.tensor_copy(
+                out=bg_wide[:], in_=bias_cols[:, D_TILES : 2 * D_TILES].unsqueeze(2).to_broadcast([P, D_TILES, P])
+            )
+            bg_spread = psum.tile([P, D_TILES, P], F32, tag="bank")
+            for m in range(D_TILES):
+                nc.tensor.transpose(bg_spread[:, m, :], bg_wide[:, m, :], ident_f32[:])
+            nc.vector.tensor_copy(out=bg_all[:], in_=bg_spread[:].rearrange("p m d -> p (m d)"))
 
         w_codes = {}
         w_planes = {}
@@ -164,60 +119,117 @@ def tile_nlgate_pa_kernel(tc, v, a, Wp, bp, Wg, bg, out_0, out_1):
             w_codes[label] = keep.tile([P, A_PASSES + Z_PASSES, D], U32, align_bytes=64, name="w%s_codes" % label)
             w_planes[label] = keep.tile([P, A_PASSES + Z_PASSES, D], U8, align_bytes=64, name="w%s_planes" % label)
 
-        def quantise_weight_half(label, h):
-            words = w_raw[(label, h)][:].bitcast(F32)
-            d_cols = slice(2 * P * h, 2 * P * (h + 1))
-            for g in range(A_PASSES + Z_PASSES):
+        def quantise_weight_half(label, half):
+            words = w_raw[(label, half)][:].bitcast(F32)
+            d_cols = slice(2 * P * half, 2 * P * (half + 1))
+            for kp in range(A_PASSES + Z_PASSES):
                 flipped = psum.tile([P, 2, 2 * P], F32, tag="bank")
                 for u in range(2):
                     for m in range(2):
-                        first = P * (2 * g + u)
+                        first = P * (2 * kp + u)
                         nc.tensor.transpose(
                             flipped[:, u, P * m : P * (m + 1)], words[:, m, first : first + P], ident_f32[:]
                         )
                 w_grouped = stage.tile([P, 2 * P, 4], BF16, align_bytes=64)
-                nc.scalar.copy(out=w_grouped[:].bitcast(F32), in_=flipped[:].rearrange("p u d -> p d u"))
+                nc.scalar.copy(
+                    out=w_grouped[:].bitcast(F32).rearrange("p (q m) u -> p q m u", m=2),
+                    in_=flipped[:].rearrange("p u (m q) -> p q m u", m=2),
+                )
                 nc.vector.quantize_mx(
-                    out=w_codes[label][:, g, d_cols].bitcast(FP8X4),
-                    scales=w_planes[label][:, g, d_cols],
+                    out=w_codes[label][:, kp, d_cols].bitcast(FP8X4),
+                    scales=w_planes[label][:, kp, d_cols],
                     in_=w_grouped[:].rearrange("p d j -> p (d j)"),
                 )
 
-        g_bias = keep.tile([P, T, D], F32)
+        z_sums = keep.tile([P, SLABS, 2 * T], F32)
 
-        def video_rows_for_g(t):
+        def fold_video():
+            for s in range(SLABS):
+                frames = v_raw[s][:].rearrange("p (f hi lo) -> p hi f lo", hi=HI, lo=LO)
+                folded = psum.tile([P, 2 * T, LO], F32, tag="bank")
+                for hi in range(HI):
+                    nc.tensor.matmul(
+                        folded[:], lhsT=ident_bf16[:], rhs=frames[:, hi], start=(hi == 0), stop=(hi == HI - 1)
+                    )
+                nc.vector.tensor_reduce(out=z_sums[:, s, :], in_=folded[:], axis=mybir.AxisListType.X, op=ADD)
+
+        z_codes = keep.tile([P, Z_PASSES, T * Z_COPIES], U32, align_bytes=64)
+        z_planes = keep.tile([P, Z_PASSES, T * Z_COPIES], U8, align_bytes=64)
+        nc.vector.memset(z_planes[:].bitcast(I32), 0)
+        z_wide_codes = keep.tile([P, Z_PASSES * CHUNKS, P], U32, align_bytes=64)
+        z_wide_planes = keep.tile([P, Z_PASSES * CHUNKS, P], U8, align_bytes=64)
+
+        def quantise_video():
+            z_grouped = keep.tile([P, Z_PASSES, T, Z_COPIES, 4], BF16, align_bytes=64)
+            for kp in range(Z_PASSES):
+                nc.vector.tensor_scalar(
+                    out=z_grouped[:, kp],
+                    in0=z_sums[:, 2 * kp : 2 * kp + 2, :]
+                    .rearrange("p u (e t) -> p t (u e)", e=2)
+                    .unsqueeze(2)
+                    .to_broadcast([P, T, Z_COPIES, 4]),
+                    scalar1=1.0 / HW,
+                    scalar2=None,
+                    op0=MULT,
+                )
+            nc.vector.quantize_mx(
+                out=z_codes[:].rearrange("p kp c -> p (kp c)").bitcast(FP8X4),
+                scales=z_planes[:].rearrange("p kp c -> p (kp c)"),
+                in_=z_grouped[:].rearrange("p kp t r j -> p (kp t r j)"),
+            )
+            repeats = P // T_PER_CHUNK // Z_COPIES
+            nc.vector.tensor_copy(
+                out=z_wide_codes[:].bitcast(I32).rearrange("p s (i b r) -> p (s i) b r", i=T_PER_CHUNK, b=repeats),
+                in_=z_codes[:]
+                .bitcast(I32)
+                .rearrange("p kp (t r) -> p (kp t) r", t=T)
+                .unsqueeze(2)
+                .to_broadcast([P, Z_PASSES * T, repeats, Z_COPIES]),
+            )
+            nc.vector.tensor_copy(
+                out=z_wide_planes[:].bitcast(I32).rearrange("p s (i b r) -> p (s i) b r", i=T_PER_CHUNK, b=repeats),
+                in_=z_planes[:]
+                .bitcast(I32)
+                .rearrange("p kp (t r) -> p (kp t) r", t=T)
+                .unsqueeze(2)
+                .to_broadcast([P, Z_PASSES * T, repeats, Z_COPIES // 4]),
+            )
+
+        g_bias = keep.tile([P, CHUNKS, D], F32)
+
+        def video_rows_for_g(c):
             z_g = psum.tile([P, D], F32, tag="bank")
-            for g in range(Z_PASSES):
+            for kp in range(Z_PASSES):
                 nc.tensor.matmul_mx(
                     out=z_g[:],
-                    lhsT=z_wide_codes[:, T * g + t, :].bitcast(FP8X4),
-                    lhsT_scale=z_wide_planes[:, T * g + t, :],
-                    rhs=w_codes["g"][:, A_PASSES + g, :].bitcast(FP8X4),
-                    rhs_scale=w_planes["g"][:, A_PASSES + g, :],
-                    start=(g == 0),
-                    stop=(g == Z_PASSES - 1),
+                    lhsT=z_wide_codes[:, CHUNKS * kp + c, :].bitcast(FP8X4),
+                    lhsT_scale=z_wide_planes[:, CHUNKS * kp + c, :],
+                    rhs=w_codes["g"][:, A_PASSES + kp, :].bitcast(FP8X4),
+                    rhs_scale=w_planes["g"][:, A_PASSES + kp, :],
+                    start=(kp == 0),
+                    stop=(kp == Z_PASSES - 1),
                 )
-            nc.vector.tensor_tensor(out=g_bias[:, t, :], in0=z_g[:], in1=bg_all[:], op=ADD)
+            nc.vector.tensor_tensor(out=g_bias[:, c, :], in0=z_g[:], in1=bg_all[:], op=ADD)
 
         phi_bias = keep.tile([P, D_TILES, T], F32)
 
         def video_columns_for_phi():
             z_phi = psum.tile([P, D_TILES, T, Z_COPIES], F32, tag="bank")
             for m in range(D_TILES):
-                for g in range(Z_PASSES):
+                for kp in range(Z_PASSES):
                     nc.tensor.matmul_mx(
                         out=z_phi[:, m],
-                        lhsT=w_codes["p"][:, A_PASSES + g, P * m : P * (m + 1)].bitcast(FP8X4),
-                        lhsT_scale=w_planes["p"][:, A_PASSES + g, P * m : P * (m + 1)],
-                        rhs=z_codes[:, g, :].bitcast(FP8X4),
-                        rhs_scale=z_planes[:, g, :],
-                        start=(g == 0),
-                        stop=(g == Z_PASSES - 1),
+                        lhsT=w_codes["p"][:, A_PASSES + kp, P * m : P * (m + 1)].bitcast(FP8X4),
+                        lhsT_scale=w_planes["p"][:, A_PASSES + kp, P * m : P * (m + 1)],
+                        rhs=z_codes[:, kp, :].bitcast(FP8X4),
+                        rhs_scale=z_planes[:, kp, :],
+                        start=(kp == 0),
+                        stop=(kp == Z_PASSES - 1),
                     )
             nc.vector.tensor_tensor(
                 out=phi_bias[:],
                 in0=z_phi[:, :, :, 0],
-                in1=bp_cols[:].unsqueeze(2).to_broadcast([P, D_TILES, T]),
+                in1=bp_cols.unsqueeze(2).to_broadcast([P, D_TILES, T]),
                 op=ADD,
             )
 
@@ -225,102 +237,88 @@ def tile_nlgate_pa_kernel(tc, v, a, Wp, bp, Wg, bg, out_0, out_1):
         a_planes = keep.tile([P, A_PASSES, N], U8, align_bytes=64)
 
         def regroup_audio(c):
-            first = N_TILE * (c % CHUNKS_PER_HALF)
-            chunk = a_raw[c // CHUNKS_PER_HALF][:, :, :, first : first + N_TILE]
             grouped = []
-            for g in range(A_PASSES):
-                rows = chunk[:, 2 * g : 2 * g + 2, :, :].rearrange("p u e (n i) -> p n (u e) i", i=4)
-                a_grouped = stage.tile([P, N_TILE, 4], BF16, align_bytes=64, bufs=2 * A_PASSES)
-                spread = a_grouped[:].rearrange("p (n i) j -> p n j i", i=4)
-                if g == 0:
-                    nc.vector.tensor_copy(out=spread, in_=rows)
+            for kp in range(A_PASSES):
+                channels = a_raw[c][:, 2 * kp : 2 * kp + 2, :, :].rearrange("p u e (q j) -> p q (u e) j", j=J)
+                a_grouped = stage.tile([P, N_TILE, 4], BF16, align_bytes=64, bufs=A_BUFS)
+                spread = a_grouped[:].rearrange("p (j q) w -> p q w j", j=J)
+                if kp == 0 or c == 0:
+                    nc.vector.tensor_copy(out=spread, in_=channels)
                 else:
-                    nc.scalar.copy(out=spread, in_=rows)
+                    nc.scalar.copy(out=spread, in_=channels)
                 grouped.append(a_grouped)
             return grouped
 
         def quantise_audio(c, grouped):
             n_cols = slice(N_TILE * c, N_TILE * (c + 1))
-            for g in range(A_PASSES):
+            for kp in range(A_PASSES):
                 nc.vector.quantize_mx(
-                    out=a_codes[:, g, n_cols].bitcast(FP8X4),
-                    scales=a_planes[:, g, n_cols],
-                    in_=grouped[g][:].rearrange("p n j -> p (n j)"),
+                    out=a_codes[:, kp, n_cols].bitcast(FP8X4),
+                    scales=a_planes[:, kp, n_cols],
+                    in_=grouped[kp][:].rearrange("p n w -> p (n w)"),
                 )
-
-        def g_tile(c, j):
-            n_rows = slice(N_TILE * c + P * j, N_TILE * c + P * (j + 1))
-            t = (N_TILE * c + P * j) // COLS_PER_T
-            g_acc = psum.tile([P, D], F32, tag="bank")
-            for g in range(A_PASSES):
-                nc.tensor.matmul_mx(
-                    out=g_acc[:],
-                    lhsT=a_codes[:, g, n_rows].bitcast(FP8X4),
-                    lhsT_scale=a_planes[:, g, n_rows],
-                    rhs=w_codes["g"][:, g, :].bitcast(FP8X4),
-                    rhs_scale=w_planes["g"][:, g, :],
-                    start=(g == 0),
-                    stop=(g == A_PASSES - 1),
-                )
-            g_out = outs.tile([P, D], F32)
-            nc.vector.tensor_tensor(out=g_out[:], in0=g_acc[:], in1=g_bias[:, t, :], op=ADD)
-            nc.sync.dma_start(out=out_1[0, n_rows, :], in_=g_out[:])
-
-        def phi_rows(h, m):
-            d_rows = slice(P * m, P * (m + 1))
-            phi_out = outs.tile([P, T_PER_HALF, COLS_PER_T], F32, bufs=PHI_BUFS)
-            for c in range(CHUNKS_PER_HALF * h, CHUNKS_PER_HALF * (h + 1)):
-                n_cols = slice(N_TILE * c, N_TILE * (c + 1))
-                phi_acc = psum.tile([P, T_PER_CHUNK, COLS_PER_T], F32, tag="bank")
-                for g in range(A_PASSES):
-                    nc.tensor.matmul_mx(
-                        out=phi_acc[:].rearrange("p t n -> p (t n)"),
-                        lhsT=w_codes["p"][:, g, d_rows].bitcast(FP8X4),
-                        lhsT_scale=w_planes["p"][:, g, d_rows],
-                        rhs=a_codes[:, g, n_cols].bitcast(FP8X4),
-                        rhs_scale=a_planes[:, g, n_cols],
-                        start=(g == 0),
-                        stop=(g == A_PASSES - 1),
-                    )
-                for i in range(T_PER_CHUNK):
-                    t = T_PER_CHUNK * c + i
-                    nc.scalar.activation(
-                        out=phi_out[:, t - T_PER_HALF * h, :],
-                        in_=phi_acc[:, i, :],
-                        func=IDENTITY,
-                        bias=phi_bias[:, m, t : t + 1],
-                    )
-            nc.sync.dma_start(
-                out=out_0[0, d_rows, HALF_COLS * h : HALF_COLS * (h + 1)],
-                in_=phi_out[:].rearrange("p t n -> p (t n)"),
-            )
 
         def g_tiles(c):
-            for j in range(N_TILE // P):
-                g_tile(c, j)
+            out_rows = out_1[0, N_TILE * c : N_TILE * (c + 1), :].rearrange("(q j) d -> q j d", j=J)
+            g_out = outs.tile([P, J, D], F32, bufs=G_BUFS)
+            for j in range(J):
+                places = slice(N_TILE * c + P * j, N_TILE * c + P * (j + 1))
+                g_acc = psum.tile([P, D], F32, tag="bank")
+                for kp in range(A_PASSES):
+                    nc.tensor.matmul_mx(
+                        out=g_acc[:],
+                        lhsT=a_codes[:, kp, places].bitcast(FP8X4),
+                        lhsT_scale=a_planes[:, kp, places],
+                        rhs=w_codes["g"][:, kp, :].bitcast(FP8X4),
+                        rhs_scale=w_planes["g"][:, kp, :],
+                        start=(kp == 0),
+                        stop=(kp == A_PASSES - 1),
+                    )
+                nc.vector.tensor_tensor(out=g_out[:, j, :], in0=g_acc[:], in1=g_bias[:, c, :], op=ADD)
+                if j % 2 == 1:
+                    nc.sync.dma_start(out=out_rows[:, j - 1 : j + 1, :], in_=g_out[:, j - 1 : j + 1, :])
 
+        def phi_tile(c, m):
+            n_cols = slice(N_TILE * c, N_TILE * (c + 1))
+            d_rows = slice(P * m, P * (m + 1))
+            phi_acc = psum.tile([P, N_TILE], F32, tag="bank")
+            for kp in range(A_PASSES):
+                nc.tensor.matmul_mx(
+                    out=phi_acc[:],
+                    lhsT=w_codes["p"][:, kp, d_rows].bitcast(FP8X4),
+                    lhsT_scale=w_planes["p"][:, kp, d_rows],
+                    rhs=a_codes[:, kp, n_cols].bitcast(FP8X4),
+                    rhs_scale=a_planes[:, kp, n_cols],
+                    start=(kp == 0),
+                    stop=(kp == A_PASSES - 1),
+                )
+            by_column = phi_acc[:].rearrange("p (j i x) -> p i x j", j=J, i=T_PER_CHUNK)
+            phi_out = outs.tile([P, T_PER_CHUNK, COLS_PER_T // J, J], F32)
+            for i in range(T_PER_CHUNK):
+                t = T_PER_CHUNK * c + i
+                nc.scalar.activation(
+                    out=phi_out[:, i], in_=by_column[:, i], func=IDENTITY, bias=phi_bias[:, m, t : t + 1]
+                )
+            nc.sync.dma_start(out=out_0[0, d_rows, n_cols], in_=phi_out[:].rearrange("p i x j -> p (i x j)"))
+
+        spread_biases()
+        fold_video()
+        quantise_video()
         quantise_weight_half("g", 0)
         quantise_weight_half("g", 1)
-        for t in range(T_PER_HALF):
-            video_rows_for_g(t)
         grouped = regroup_audio(0)
         quantise_audio(0, grouped)
-        grouped = regroup_audio(1)
-        g_tiles(0)
-        quantise_audio(1, grouped)
-        g_tiles(1)
         quantise_weight_half("p", 0)
         quantise_weight_half("p", 1)
-        video_columns_for_phi()
-        for t in range(T_PER_HALF, T):
-            video_rows_for_g(t)
-        grouped = regroup_audio(2)
-        quantise_audio(2, grouped)
-        for m in range(D_TILES):
-            phi_rows(0, m)
-        grouped = regroup_audio(3)
-        g_tiles(2)
-        quantise_audio(3, grouped)
-        g_tiles(3)
-        for m in range(D_TILES):
-            phi_rows(1, m)
+        video_rows_for_g(0)
+        for c in range(CHUNKS):
+            if c + 1 < CHUNKS:
+                grouped = regroup_audio(c + 1)
+            g_tiles(c)
+            if c + 1 < CHUNKS:
+                quantise_audio(c + 1, grouped)
+                video_rows_for_g(c + 1)
+            if c == 0:
+                video_columns_for_phi()
+            for m in range(D_TILES):
+                phi_tile(c, m)

@@ -52,7 +52,7 @@ def tile_nlgate_pa_kernel(tc, v, a, Wp, bp, Wg, bg, out_0, out_1):
         ctx.enter_context(tc.manual_schedule())
 
         bias_rows = const.tile([P, P], BF16)
-        nc.vector.memset(bias_rows[:], 0.0)
+        nc.gpsimd.memset(bias_rows[:], 0.0)
         nc.sync.dma_start(out=bias_rows[0:D_TILES, :], in_=bp.rearrange("(m p) -> m p", p=P))
         nc.sync.dma_start(out=bias_rows[D_TILES : 2 * D_TILES, :], in_=bg.rearrange("(m p) -> m p", p=P))
 
@@ -77,19 +77,20 @@ def tile_nlgate_pa_kernel(tc, v, a, Wp, bp, Wg, bg, out_0, out_1):
         a_slabs = a.rearrange("b (s p e) at af -> p (b s) e (at af)", s=SLABS, p=P, e=2)
         a_raw = []
 
-        def load_audio(c):
-            a_chunk = keep.tile([P, SLABS, 2, N_TILE], BF16, name="a_raw%d" % c)
+        def load_audio(c, chunks):
+            a_cols = keep.tile([P, SLABS, 2, N_TILE * chunks], BF16, name="a_raw%d" % c)
             for s in range(SLABS):
                 nc.sync.dma_start(
-                    out=a_chunk[:, s, :, :], in_=a_slabs[:, s, :, N_TILE * c : N_TILE * (c + 1)]
+                    out=a_cols[:, s, :, :], in_=a_slabs[:, s, :, N_TILE * c : N_TILE * (c + chunks)]
                 )
-            a_raw.append(a_chunk)
+            for i in range(chunks):
+                a_raw.append(a_cols[:, :, :, N_TILE * i : N_TILE * (i + 1)])
 
         load_weight("g", Wg)
-        load_audio(0)
+        load_audio(0, 1)
         load_weight("p", Wp)
-        for c in range(1, CHUNKS):
-            load_audio(c)
+        load_audio(1, 1)
+        load_audio(2, 2)
 
         ident_bf16 = const.tile([P, P], BF16)
         make_identity(nc, ident_bf16[:])

@@ -30,8 +30,8 @@ D_TILES = D // P
 LO = 32
 HI = HW // LO
 PHI_BUFS = 8
-G_BUFS = 3
-W_BUFS = 5
+G_BUFS = 10
+W_BUFS = 4
 A_BUFS = 2 * A_PASSES
 PSUM_BANKS = 8
 Z_COPIES = 16
@@ -157,8 +157,8 @@ def tile_nlgate_pa_kernel(tc, v, a, Wp, bp, Wg, bg, out_0, out_1):
         z_codes = keep.tile([P, Z_PASSES, T * Z_COPIES], U32, align_bytes=64)
         z_planes = keep.tile([P, Z_PASSES, T * Z_COPIES], U8, align_bytes=64)
         nc.vector.memset(z_planes[:].bitcast(I32), 0)
-        z_wide_codes = keep.tile([P, Z_PASSES * CHUNKS, P], U32, align_bytes=64)
-        z_wide_planes = keep.tile([P, Z_PASSES * CHUNKS, P], U8, align_bytes=64)
+        z_wide_codes = keep.tile([P, Z_PASSES * T, P], U32, align_bytes=64)
+        z_wide_planes = keep.tile([P, Z_PASSES * T, P], U8, align_bytes=64)
 
         def quantise_video():
             z_grouped = keep.tile([P, Z_PASSES, T, Z_COPIES, 4], BF16, align_bytes=64)
@@ -178,9 +178,9 @@ def tile_nlgate_pa_kernel(tc, v, a, Wp, bp, Wg, bg, out_0, out_1):
                 scales=z_planes[:].rearrange("p kp c -> p (kp c)"),
                 in_=z_grouped[:].rearrange("p kp t r j -> p (kp t r j)"),
             )
-            repeats = P // T_PER_CHUNK // Z_COPIES
+            repeats = P // Z_COPIES
             nc.vector.tensor_copy(
-                out=z_wide_codes[:].bitcast(I32).rearrange("p s (i b r) -> p (s i) b r", i=T_PER_CHUNK, b=repeats),
+                out=z_wide_codes[:].bitcast(I32).rearrange("p s (b r) -> p s b r", b=repeats),
                 in_=z_codes[:]
                 .bitcast(I32)
                 .rearrange("p kp (t r) -> p (kp t) r", t=T)
@@ -188,7 +188,7 @@ def tile_nlgate_pa_kernel(tc, v, a, Wp, bp, Wg, bg, out_0, out_1):
                 .to_broadcast([P, Z_PASSES * T, repeats, Z_COPIES]),
             )
             nc.vector.tensor_copy(
-                out=z_wide_planes[:].bitcast(I32).rearrange("p s (i b r) -> p (s i) b r", i=T_PER_CHUNK, b=repeats),
+                out=z_wide_planes[:].bitcast(I32).rearrange("p s (b r) -> p s b r", b=repeats),
                 in_=z_planes[:]
                 .bitcast(I32)
                 .rearrange("p kp (t r) -> p (kp t) r", t=T)
@@ -196,21 +196,22 @@ def tile_nlgate_pa_kernel(tc, v, a, Wp, bp, Wg, bg, out_0, out_1):
                 .to_broadcast([P, Z_PASSES * T, repeats, Z_COPIES // 4]),
             )
 
-        g_bias = keep.tile([P, CHUNKS, D], F32)
+        g_bias = keep.tile([P, T, D], F32)
 
         def video_rows_for_g(c):
-            z_g = psum.tile([P, D], F32, tag="bank")
-            for kp in range(Z_PASSES):
-                nc.tensor.matmul_mx(
-                    out=z_g[:],
-                    lhsT=z_wide_codes[:, CHUNKS * kp + c, :].bitcast(FP8X4),
-                    lhsT_scale=z_wide_planes[:, CHUNKS * kp + c, :],
-                    rhs=w_codes["g"][:, A_PASSES + kp, :].bitcast(FP8X4),
-                    rhs_scale=w_planes["g"][:, A_PASSES + kp, :],
-                    start=(kp == 0),
-                    stop=(kp == Z_PASSES - 1),
-                )
-            nc.vector.tensor_tensor(out=g_bias[:, c, :], in0=z_g[:], in1=bg_all[:], op=ADD)
+            for t in range(T_PER_CHUNK * c, T_PER_CHUNK * (c + 1)):
+                z_g = psum.tile([P, D], F32, tag="bank")
+                for kp in range(Z_PASSES):
+                    nc.tensor.matmul_mx(
+                        out=z_g[:],
+                        lhsT=z_wide_codes[:, T * kp + t, :].bitcast(FP8X4),
+                        lhsT_scale=z_wide_planes[:, T * kp + t, :],
+                        rhs=w_codes["g"][:, A_PASSES + kp, :].bitcast(FP8X4),
+                        rhs_scale=w_planes["g"][:, A_PASSES + kp, :],
+                        start=(kp == 0),
+                        stop=(kp == Z_PASSES - 1),
+                    )
+                nc.vector.tensor_tensor(out=g_bias[:, t, :], in0=z_g[:], in1=bg_all[:], op=ADD)
 
         phi_bias = keep.tile([P, D_TILES, T], F32)
 
@@ -240,9 +241,9 @@ def tile_nlgate_pa_kernel(tc, v, a, Wp, bp, Wg, bg, out_0, out_1):
         def regroup_audio(c):
             grouped = []
             for kp in range(A_PASSES):
-                channels = a_raw[c][:, 2 * kp : 2 * kp + 2, :, :].rearrange("p u e (q j) -> p q (u e) j", j=J)
+                channels = a_raw[c][:, 2 * kp : 2 * kp + 2, :, :].rearrange("p u e (n i) -> p n (u e) i", i=4)
                 a_grouped = stage.tile([P, N_TILE, 4], BF16, align_bytes=64, bufs=A_BUFS)
-                spread = a_grouped[:].rearrange("p (j q) w -> p q w j", j=J)
+                spread = a_grouped[:].rearrange("p (n i) w -> p n w i", i=4)
                 if kp == 0 or c == 0:
                     nc.vector.tensor_copy(out=spread, in_=channels)
                 else:
@@ -260,32 +261,31 @@ def tile_nlgate_pa_kernel(tc, v, a, Wp, bp, Wg, bg, out_0, out_1):
                 )
 
         def g_tiles(c):
-            out_rows = out_1[0, N_TILE * c : N_TILE * (c + 1), :].rearrange("(q j) d -> q j d", j=J)
-            g_out = outs.tile([P, J, D], F32, bufs=G_BUFS)
             for j in range(J):
-                places = slice(N_TILE * c + P * j, N_TILE * c + P * (j + 1))
+                n_rows = slice(N_TILE * c + P * j, N_TILE * c + P * (j + 1))
+                t = (N_TILE * c + P * j) // COLS_PER_T
                 g_acc = psum.tile([P, D], F32, tag="bank")
                 for kp in range(A_PASSES):
                     nc.tensor.matmul_mx(
                         out=g_acc[:],
-                        lhsT=a_codes[:, kp, places].bitcast(FP8X4),
-                        lhsT_scale=a_planes[:, kp, places],
+                        lhsT=a_codes[:, kp, n_rows].bitcast(FP8X4),
+                        lhsT_scale=a_planes[:, kp, n_rows],
                         rhs=w_codes["g"][:, kp, :].bitcast(FP8X4),
                         rhs_scale=w_planes["g"][:, kp, :],
                         start=(kp == 0),
                         stop=(kp == A_PASSES - 1),
                     )
-                nc.vector.tensor_tensor(out=g_out[:, j, :], in0=g_acc[:], in1=g_bias[:, c, :], op=ADD)
-                if j % 2 == 1:
-                    nc.sync.dma_start(out=out_rows[:, j - 1 : j + 1, :], in_=g_out[:, j - 1 : j + 1, :])
+                g_out = outs.tile([P, D], F32, bufs=G_BUFS)
+                nc.vector.tensor_tensor(out=g_out[:], in0=g_acc[:], in1=g_bias[:, t, :], op=ADD)
+                nc.sync.dma_start(out=out_1[0, n_rows, :], in_=g_out[:])
 
         def phi_tile(c, m):
             n_cols = slice(N_TILE * c, N_TILE * (c + 1))
             d_rows = slice(P * m, P * (m + 1))
-            phi_acc = psum.tile([P, N_TILE], F32, tag="bank")
+            phi_acc = psum.tile([P, T_PER_CHUNK, COLS_PER_T], F32, tag="bank")
             for kp in range(A_PASSES):
                 nc.tensor.matmul_mx(
-                    out=phi_acc[:],
+                    out=phi_acc[:].rearrange("p i n -> p (i n)"),
                     lhsT=w_codes["p"][:, kp, d_rows].bitcast(FP8X4),
                     lhsT_scale=w_planes["p"][:, kp, d_rows],
                     rhs=a_codes[:, kp, n_cols].bitcast(FP8X4),
@@ -293,14 +293,13 @@ def tile_nlgate_pa_kernel(tc, v, a, Wp, bp, Wg, bg, out_0, out_1):
                     start=(kp == 0),
                     stop=(kp == A_PASSES - 1),
                 )
-            by_column = phi_acc[:].rearrange("p (j i x) -> p i x j", j=J, i=T_PER_CHUNK)
-            phi_out = outs.tile([P, T_PER_CHUNK, COLS_PER_T // J, J], F32)
+            phi_out = outs.tile([P, T_PER_CHUNK, COLS_PER_T], F32)
             for i in range(T_PER_CHUNK):
                 t = T_PER_CHUNK * c + i
                 nc.scalar.activation(
-                    out=phi_out[:, i], in_=by_column[:, i], func=IDENTITY, bias=phi_bias[:, m, t : t + 1]
+                    out=phi_out[:, i], in_=phi_acc[:, i], func=IDENTITY, bias=phi_bias[:, m, t : t + 1]
                 )
-            nc.sync.dma_start(out=out_0[0, d_rows, n_cols], in_=phi_out[:].rearrange("p i x j -> p (i x j)"))
+            nc.sync.dma_start(out=out_0[0, d_rows, n_cols], in_=phi_out[:].rearrange("p i n -> p (i n)"))
 
         spread_biases()
         fold_video()

from contextlib import ExitStack

import concourse.mybir as mybir
from concourse.masks import make_identity

F32 = mybir.dt.float32
BF16 = mybir.dt.bfloat16
I32 = mybir.dt.int32
U32 = mybir.dt.uint32
U8 = mybir.dt.uint8
FP8X4 = mybir.dt.float8_e4m3fn_x4
ADD = mybir.AluOpType.add
MULT = mybir.AluOpType.mult
IDENTITY = mybir.ActivationFunctionType.Identity

P = 128
C = 1024
T = 8
HW = 256
N = 2048
COLS_PER_T = N // T
D = 512
K_PASS = 512
A_PASSES = C // K_PASS
Z_PASSES = C // K_PASS
SLABS = C // (2 * P)
N_TILE = 512
CHUNKS = N // N_TILE
D_TILES = D // P
LO = 32
HI = HW // LO
PHI_BUFS = 8
G_BUFS = 10
W_BUFS = 4
A_BUFS = 2 * A_PASSES
PSUM_BANKS = 8
Z_COPIES = 16
T_PER_CHUNK = N_TILE // COLS_PER_T
J = N_TILE // P

FLOPS = 2 * 2 * D * (2 * C) * N


def tile_nlgate_pa_kernel(tc, v, a, Wp, bp, Wg, bg, out_0, out_1):
    nc = tc.nc
    with ExitStack() as ctx:
        const = ctx.enter_context(tc.tile_pool(name="const", bufs=1))
        keep = ctx.enter_context(tc.tile_pool(name="keep", bufs=1))
        stage = ctx.enter_context(tc.tile_pool(name="stage", bufs=W_BUFS))
        outs = ctx.enter_context(tc.tile_pool(name="outs", bufs=PHI_BUFS))
        psum = ctx.enter_context(tc.psum_pool(name="psum", bufs=PSUM_BANKS))
        ctx.enter_context(tc.manual_schedule())

        bias_rows = const.tile([P, P], BF16)
        nc.gpsimd.memset(bias_rows[:], 0.0)
        nc.sync.dma_start(out=bias_rows[0:D_TILES, :], in_=bp.rearrange("(m p) -> m p", p=P))
        nc.sync.dma_start(out=bias_rows[D_TILES : 2 * D_TILES, :], in_=bg.rearrange("(m p) -> m p", p=P))

        v_slabs = v.rearrange("b (s p e) t h w -> p (b s) (e t h w)", s=SLABS, p=P, e=2)
        v_raw = []
        for s in range(SLABS):
            v_slab = keep.tile([P, 2 * T * HW], BF16, name="v_raw%d" % s)
            nc.sync.dma_start(out=v_slab[:], in_=v_slabs[:, s, :])
            v_raw.append(v_slab)

        w_raw = {}

        def load_weight(label, w):
            for half in range(2):
                w_half = keep.tile([P, 2, 2 * C], BF16, name="w%s_raw%d" % (label, half))
                nc.sync.dma_start(
                    out=w_half[:],
                    in_=w[2 * P * half : 2 * P * (half + 1), :].rearrange("(p m) k -> p m k", m=2),
                )
                w_raw[(label, half)] = w_half

        a_slabs = a.rearrange("b (s p e) at af -> p (b s) e (at af)", s=SLABS, p=P, e=2)
        a_raw = []

        def load_audio(c, chunks):
            a_cols = keep.tile([P, SLABS, 2, N_TILE * chunks], BF16, name="a_raw%d" % c)
            for s in range(SLABS):
                nc.sync.dma_start(
                    out=a_cols[:, s, :, :], in_=a_slabs[:, s, :, N_TILE * c : N_TILE * (c + chunks)]
                )
            for i in range(chunks):
                a_raw.append(a_cols[:, :, :, N_TILE * i : N_TILE * (i + 1)])

        load_weight("g", Wg)
        load_audio(0, 1)
        load_weight("p", Wp)
        load_audio(1, 1)
        load_audio(2, 2)

        ident_bf16 = const.tile([P, P], BF16)
        make_identity(nc, ident_bf16[:])
        ident_f32 = const.tile([P, P], F32)
        make_identity(nc, ident_f32[:])

        bias_cols = const.tile([P, 2 * D_TILES], F32)
        bp_cols = bias_cols[:, 0:D_TILES]
        bg_all = const.tile([P, D], F32)

        def spread_biases():
            bias_flipped = psum.tile([P, P], BF16, tag="bank")
            nc.tensor.transpose(bias_flipped[:], bias_rows[:], ident_bf16[:])
            nc.vector.tensor_copy(out=bias_cols[:], in_=bias_flipped[:, 0 : 2 * D_TILES])
            bg_wide = const.tile([P, D_TILES, P], F32)
            nc.vector.tensor_copy(
                out=bg_wide[:], in_=bias_cols[:, D_TILES : 2 * D_TILES].unsqueeze(2).to_broadcast([P, D_TILES, P])
            )
            bg_spread = psum.tile([P, D_TILES, P], F32, tag="bank")
            for m in range(D_TILES):
                nc.tensor.transpose(bg_spread[:, m, :], bg_wide[:, m, :], ident_f32[:])
            nc.vector.tensor_copy(out=bg_all[:], in_=bg_spread[:].rearrange("p m d -> p (m d)"))

        w_codes = {}
        w_planes = {}
        for label in ("g", "p"):
            w_codes[label] = keep.tile([P, A_PASSES + Z_PASSES, D], U32, align_bytes=64, name="w%s_codes" % label)
            w_planes[label] = keep.tile([P, A_PASSES + Z_PASSES, D], U8, align_bytes=64, name="w%s_planes" % label)

        def quantise_weight_half(label, half):
            words = w_raw[(label, half)][:].bitcast(F32)
            d_cols = slice(2 * P * half, 2 * P * (half + 1))
            for kp in range(A_PASSES + Z_PASSES):
                flipped = psum.tile([P, 2, 2 * P], F32, tag="bank")
                for u in range(2):
                    for m in range(2):
                        first = P * (2 * kp + u)
                        nc.tensor.transpose(
                            flipped[:, u, P * m : P * (m + 1)], words[:, m, first : first + P], ident_f32[:]
                        )
                w_grouped = stage.tile([P, 2 * P, 4], BF16, align_bytes=64)
                nc.scalar.copy(
                    out=w_grouped[:].bitcast(F32).rearrange("p (q m) u -> p q m u", m=2),
                    in_=flipped[:].rearrange("p u (m q) -> p q m u", m=2),
                )
                nc.vector.quantize_mx(
                    out=w_codes[label][:, kp, d_cols].bitcast(FP8X4),
                    scales=w_planes[label][:, kp, d_cols],
                    in_=w_grouped[:].rearrange("p d j -> p (d j)"),
                )

        z_sums = keep.tile([P, SLABS, 2 * T], F32)

        def fold_video():
            for s in range(SLABS):
                frames = v_raw[s][:].rearrange("p (f hi lo) -> p hi f lo", hi=HI, lo=LO)
                folded = psum.tile([P, 2 * T, LO], F32, tag="bank")
                for hi in range(HI):
                    nc.tensor.matmul(
                        folded[:], lhsT=ident_bf16[:], rhs=frames[:, hi], start=(hi == 0), stop=(hi == HI - 1)
                    )
                nc.vector.tensor_reduce(out=z_sums[:, s, :], in_=folded[:], axis=mybir.AxisListType.X, op=ADD)

        z_codes = keep.tile([P, Z_PASSES, T * Z_COPIES], U32, align_bytes=64)
        z_planes = keep.tile([P, Z_PASSES, T * Z_COPIES], U8, align_bytes=64)
        nc.vector.memset(z_planes[:].bitcast(I32), 0)
        z_wide_codes = keep.tile([P, Z_PASSES * T, P], U32, align_bytes=64)
        z_wide_planes = keep.tile([P, Z_PASSES * T, P], U8, align_bytes=64)

        def quantise_video():
            z_grouped = keep.tile([P, Z_PASSES, T, Z_COPIES, 4], BF16, align_bytes=64)
            for kp in range(Z_PASSES):
                nc.vector.tensor_scalar(
                    out=z_grouped[:, kp],
                    in0=z_sums[:, 2 * kp : 2 * kp + 2, :]
                    .rearrange("p u (e t) -> p t (u e)", e=2)
                    .unsqueeze(2)
                    .to_broadcast([P, T, Z_COPIES, 4]),
                    scalar1=1.0 / HW,
                    scalar2=None,
                    op0=MULT,
                )
            nc.vector.quantize_mx(
                out=z_codes[:].rearrange("p kp c -> p (kp c)").bitcast(FP8X4),
                scales=z_planes[:].rearrange("p kp c -> p (kp c)"),
                in_=z_grouped[:].rearrange("p kp t r j -> p (kp t r j)"),
            )
            repeats = P // Z_COPIES
            nc.vector.tensor_copy(
                out=z_wide_codes[:].bitcast(I32).rearrange("p s (b r) -> p s b r", b=repeats),
                in_=z_codes[:]
                .bitcast(I32)
                .rearrange("p kp (t r) -> p (kp t) r", t=T)
                .unsqueeze(2)
                .to_broadcast([P, Z_PASSES * T, repeats, Z_COPIES]),
            )
            nc.vector.tensor_copy(
                out=z_wide_planes[:].bitcast(I32).rearrange("p s (b r) -> p s b r", b=repeats),
                in_=z_planes[:]
                .bitcast(I32)
                .rearrange("p kp (t r) -> p (kp t) r", t=T)
                .unsqueeze(2)
                .to_broadcast([P, Z_PASSES * T, repeats, Z_COPIES // 4]),
            )

        g_bias = keep.tile([P, T, D], F32)

        def video_rows_for_g(c):
            for t in range(T_PER_CHUNK * c, T_PER_CHUNK * (c + 1)):
                z_g = psum.tile([P, D], F32, tag="bank")
                for kp in range(Z_PASSES):
                    nc.tensor.matmul_mx(
                        out=z_g[:],
                        lhsT=z_wide_codes[:, T * kp + t, :].bitcast(FP8X4),
                        lhsT_scale=z_wide_planes[:, T * kp + t, :],
                        rhs=w_codes["g"][:, A_PASSES + kp, :].bitcast(FP8X4),
                        rhs_scale=w_planes["g"][:, A_PASSES + kp, :],
                        start=(kp == 0),
                        stop=(kp == Z_PASSES - 1),
                    )
                nc.vector.tensor_tensor(out=g_bias[:, t, :], in0=z_g[:], in1=bg_all[:], op=ADD)

        phi_bias = keep.tile([P, D_TILES, T], F32)

        def video_columns_for_phi():
            z_phi = psum.tile([P, D_TILES, T, Z_COPIES], F32, tag="bank")
            for m in range(D_TILES):
                for kp in range(Z_PASSES):
                    nc.tensor.matmul_mx(
                        out=z_phi[:, m],
                        lhsT=w_codes["p"][:, A_PASSES + kp, P * m : P * (m + 1)].bitcast(FP8X4),
                        lhsT_scale=w_planes["p"][:, A_PASSES + kp, P * m : P * (m + 1)],
                        rhs=z_codes[:, kp, :].bitcast(FP8X4),
                        rhs_scale=z_planes[:, kp, :],
                        start=(kp == 0),
                        stop=(kp == Z_PASSES - 1),
                    )
            nc.vector.tensor_tensor(
                out=phi_bias[:],
                in0=z_phi[:, :, :, 0],
                in1=bp_cols.unsqueeze(2).to_broadcast([P, D_TILES, T]),
                op=ADD,
            )

        a_codes = keep.tile([P, A_PASSES, N], U32, align_bytes=64)
        a_planes = keep.tile([P, A_PASSES, N], U8, align_bytes=64)

        def regroup_audio(c):
            grouped = []
            for kp in range(A_PASSES):
                channels = a_raw[c][:, 2 * kp : 2 * kp + 2, :, :].rearrange("p u e (n i) -> p n (u e) i", i=4)
                a_grouped = stage.tile([P, N_TILE, 4], BF16, align_bytes=64, bufs=A_BUFS)
                spread = a_grouped[:].rearrange("p (n i) w -> p n w i", i=4)
                if kp == 0 or c == 0:
                    nc.vector.tensor_copy(out=spread, in_=channels)
                else:
                    nc.scalar.copy(out=spread, in_=channels)
                grouped.append(a_grouped)
            return grouped

        def quantise_audio(c, grouped):
            n_cols = slice(N_TILE * c, N_TILE * (c + 1))
            for kp in range(A_PASSES):
                nc.vector.quantize_mx(
                    out=a_codes[:, kp, n_cols].bitcast(FP8X4),
                    scales=a_planes[:, kp, n_cols],
                    in_=grouped[kp][:].rearrange("p n w -> p (n w)"),
                )

        def g_tiles(c):
            for j in range(J):
                n_rows = slice(N_TILE * c + P * j, N_TILE * c + P * (j + 1))
                t = (N_TILE * c + P * j) // COLS_PER_T
                g_acc = psum.tile([P, D], F32, tag="bank")
                for kp in range(A_PASSES):
                    nc.tensor.matmul_mx(
                        out=g_acc[:],
                        lhsT=a_codes[:, kp, n_rows].bitcast(FP8X4),
                        lhsT_scale=a_planes[:, kp, n_rows],
                        rhs=w_codes["g"][:, kp, :].bitcast(FP8X4),
                        rhs_scale=w_planes["g"][:, kp, :],
                        start=(kp == 0),
                        stop=(kp == A_PASSES - 1),
                    )
                g_out = outs.tile([P, D], F32, bufs=G_BUFS)
                nc.vector.tensor_tensor(out=g_out[:], in0=g_acc[:], in1=g_bias[:, t, :], op=ADD)
                nc.sync.dma_start(out=out_1[0, n_rows, :], in_=g_out[:])

        def phi_tile(c, m):
            n_cols = slice(N_TILE * c, N_TILE * (c + 1))
            d_rows = slice(P * m, P * (m + 1))
            phi_acc = psum.tile([P, T_PER_CHUNK, COLS_PER_T], F32, tag="bank")
            for kp in range(A_PASSES):
                nc.tensor.matmul_mx(
                    out=phi_acc[:].rearrange("p i n -> p (i n)"),
                    lhsT=w_codes["p"][:, kp, d_rows].bitcast(FP8X4),
                    lhsT_scale=w_planes["p"][:, kp, d_rows],
                    rhs=a_codes[:, kp, n_cols].bitcast(FP8X4),
                    rhs_scale=a_planes[:, kp, n_cols],
                    start=(kp == 0),
                    stop=(kp == A_PASSES - 1),
                )
            phi_out = outs.tile([P, T_PER_CHUNK, COLS_PER_T], F32)
            for i in range(T_PER_CHUNK):
                t = T_PER_CHUNK * c + i
                nc.scalar.activation(
                    out=phi_out[:, i], in_=phi_acc[:, i], func=IDENTITY, bias=phi_bias[:, m, t : t + 1]
                )
            nc.sync.dma_start(out=out_0[0, d_rows, n_cols], in_=phi_out[:].rearrange("p i n -> p (i n)"))

        spread_biases()
        fold_video()
        quantise_video()
        quantise_weight_half("g", 0)
        quantise_weight_half("g", 1)
        grouped = regroup_audio(0)
        quantise_audio(0, grouped)
        quantise_weight_half("p", 0)
        quantise_weight_half("p", 1)
        video_rows_for_g(0)
        for c in range(CHUNKS):
            if c + 1 < CHUNKS:
                grouped = regroup_audio(c + 1)
            g_tiles(c)
            if c + 1 < CHUNKS:
                quantise_audio(c + 1, grouped)
                video_rows_for_g(c + 1)
            if c == 0:
                video_columns_for_phi()
            for m in range(D_TILES):
                phi_tile(c, m)
